import numpy as np
import ml_dtypes

BF16 = ml_dtypes.bfloat16


def bf(x):
    return np.asarray(x, np.float32).astype(BF16)


def f32(x):
    return np.asarray(x, np.float32)


def f64(x):
    return np.asarray(x).astype(np.float64)


def striped(idx):
    return np.tile(idx.reshape(-1, 16).T, (8, 1))


C, S, N = 256, 2048, 1024


def setup_inputs():
    table = f32(np.random.standard_normal((C, S)))
    nb = bf(4.0 * np.random.standard_normal((N, C)) / np.sqrt(N))
    dist = f32(np.random.uniform(size=(N, N)))
    cut = np.random.uniform(size=(N, N)) * (np.random.uniform(size=(N, N)) < 0.5)
    np.fill_diagonal(cut, 0.0)
    cut = f32(cut)
    relw = f32(np.random.standard_normal((C, 1)))
    w1b = bf(np.random.standard_normal((C, C)) / np.sqrt(C))
    b1 = f32(0.1 * np.random.standard_normal((C, 1)))
    return {"table": table, "nb": nb, "dist": dist, "cut": cut, "relw": relw, "w1b": w1b, "b1": b1, "offs": striped(np.random.permutation(S)[:N])}


def reference(table, nb, dist, cut, relw, w1b, b1, offs):
    idx = offs[:16].T.reshape(-1)
    e = f64(dist) * f64(cut)
    nf = (f64(nb).T @ e) * f64(relw)
    q = f64(w1b).T @ nf + f64(b1)
    return f64(table)[:, idx] + q

@@ -1,0 +1,99 @@
+import concourse.mybir as mybir
+
+F32 = mybir.dt.float32
+BF16 = mybir.dt.bfloat16
+U16 = mybir.dt.uint16
+MULT = mybir.AluOpType.mult
+ADD = mybir.AluOpType.add
+IDENTITY = mybir.ActivationFunctionType.Identity
+
+P = 128
+C = 256
+S = 2048
+N = 1024
+CB = C // P
+TB = N // P
+W = 512
+CHUNKS = N // W
+TG = 4
+GROUPS = TB // TG
+
+FLOPS = 2 * N * N * C + 2 * C * C * N
+
+
+def tile_nodescalarfeatinit_kernel(tc, table, nb, dist, cut, relw, w1b, b1, offs, out):
+    nc = tc.nc
+    dist_rows = dist.rearrange("(tb p) j -> p tb j", p=P)
+    cut_rows = cut.rearrange("(tb p) j -> p tb j", p=P)
+
+    with (
+        tc.tile_pool(name="held", bufs=1) as held,
+        tc.psum_pool(name="nf_banks", bufs=2) as nf_banks,
+        tc.psum_pool(name="q_banks", bufs=4) as q_banks,
+    ):
+        offsets = held.tile([P, N // 16], U16, name="offsets")
+        nc.sync.dma_start(offsets[:], offs)
+        nb_sb = held.tile([P, TB, C], BF16, name="nb_sb")
+        nc.scalar.dma_start(nb_sb[:], nb.rearrange("(tb p) d -> p tb d", p=P))
+        w1b_sb = held.tile([P, CB, C], BF16, name="w1b_sb")
+        nc.gpsimd.dma_start(w1b_sb[:], w1b.rearrange("(db p) c -> p db c", p=P))
+        relw_sb = held.tile([P, CB], F32, name="relw_sb")
+        b1_sb = held.tile([P, CB], F32, name="b1_sb")
+        with nc.allow_non_contiguous_dma(reason="one float32 to a partition, 256 in all"):
+            nc.gpsimd.dma_start(relw_sb[:], relw.rearrange("(db p) o -> p (db o)", p=P))
+            nc.gpsimd.dma_start(b1_sb[:], b1.rearrange("(cb p) o -> p (cb o)", p=P))
+
+        dist_sb, cut_sb, table_sb = {}, {}, []
+        for ch in range(CHUNKS):
+            cols = slice(ch * W, (ch + 1) * W)
+            for g in range(GROUPS):
+                blocks = slice(g * TG, (g + 1) * TG)
+                dist_sb[ch, g] = held.tile([P, TG, W], F32, name=f"dist{ch}_{g}")
+                nc.sync.dma_start(dist_sb[ch, g][:], dist_rows[:, blocks, cols])
+                cut_sb[ch, g] = held.tile([P, TG, W], F32, name=f"cut{ch}_{g}")
+                nc.scalar.dma_start(cut_sb[ch, g][:], cut_rows[:, blocks, cols])
+            if ch == 0:
+                for cb, queue in zip(range(CB), (nc.sync, nc.scalar)):
+                    table_sb.append(held.tile([P, S], F32, name=f"table{cb}"))
+                    queue.dma_start(table_sb[cb][:], table[cb * P : (cb + 1) * P, :])
+
+        for ch in range(CHUNKS):
+            cols = slice(ch * W, (ch + 1) * W)
+
+            nf_ps = [nf_banks.tile([P, W], F32, name=f"nf_ps{db}") for db in range(CB)]
+            for g in range(GROUPS):
+                e = held.tile([P, TG, W], BF16, name=f"e{ch}_{g}")
+                for k in range(TG):
+                    tb = g * TG + k
+                    nc.vector.tensor_tensor(e[:, k, :], dist_sb[ch, g][:, k, :], cut_sb[ch, g][:, k, :], MULT)
+                    for db in range(CB):
+                        nc.tensor.matmul(
+                            nf_ps[db][:],
+                            nb_sb[:, tb, db * P : (db + 1) * P],
+                            e[:, k, :],
+                            start=(tb == 0),
+                            stop=(tb == TB - 1),
+                        )
+
+            nf_sb = []
+            for db in range(CB):
+                nf_sb.append(held.tile([P, W], BF16, name=f"nf{ch}_{db}"))
+                nc.scalar.activation(nf_sb[db][:], nf_ps[db][:], IDENTITY, scale=relw_sb[:, db : db + 1])
+
+            for cb in range(CB):
+                q_ps = q_banks.tile([P, W], F32, name="q_ps")
+                for db in range(CB):
+                    nc.tensor.matmul(
+                        q_ps[:],
+                        w1b_sb[:, db, cb * P : (cb + 1) * P],
+                        nf_sb[db][:],
+                        start=(db == 0),
+                        stop=(db == CB - 1),
+                    )
+                q_sb = held.tile([P, W], F32, name=f"q{ch}_{cb}")
+                nc.scalar.activation(q_sb[:], q_ps[:], IDENTITY, bias=b1_sb[:, cb : cb + 1])
+
+                picked = table_sb[cb][:].indirect(offsets[:, ch * (W // 16) : (ch + 1) * (W // 16)])
+                res = held.tile([P, W], F32, name=f"res{ch}_{cb}")
+                nc.vector.tensor_tensor(res[:], picked, q_sb[:], ADD)
+                nc.sync.dma_start(out[cb * P : (cb + 1) * P, cols], res[:])

@@ -13,7 +13,7 @@ S = 2048
 N = 1024
 CB = C // P
 TB = N // P
-W = 512
+W = 256
 CHUNKS = N // W
 TG = 4
 GROUPS = TB // TG
@@ -33,17 +33,17 @@ def tile_nodescalarfeatinit_kernel(tc, table, nb, dist, cut, relw, w1b, b1, offs
     ):
         offsets = held.tile([P, N // 16], U16, name="offsets")
         nc.sync.dma_start(offsets[:], offs)
-        nb_sb = held.tile([P, TB, C], BF16, name="nb_sb")
-        nc.scalar.dma_start(nb_sb[:], nb.rearrange("(tb p) d -> p tb d", p=P))
-        w1b_sb = held.tile([P, CB, C], BF16, name="w1b_sb")
-        nc.gpsimd.dma_start(w1b_sb[:], w1b.rearrange("(db p) c -> p db c", p=P))
         relw_sb = held.tile([P, CB], F32, name="relw_sb")
         b1_sb = held.tile([P, CB], F32, name="b1_sb")
         with nc.allow_non_contiguous_dma(reason="one float32 to a partition, 256 in all"):
-            nc.gpsimd.dma_start(relw_sb[:], relw.rearrange("(db p) o -> p (db o)", p=P))
-            nc.gpsimd.dma_start(b1_sb[:], b1.rearrange("(cb p) o -> p (cb o)", p=P))
+            nc.sync.dma_start(relw_sb[:], relw.rearrange("(db p) o -> p (db o)", p=P))
+            nc.sync.dma_start(b1_sb[:], b1.rearrange("(cb p) o -> p (cb o)", p=P))
+        nb_sb = held.tile([P, TB, C], BF16, name="nb_sb")
+        nc.sync.dma_start(nb_sb[:], nb.rearrange("(tb p) d -> p tb d", p=P))
+        w1b_sb = held.tile([P, CB, C], BF16, name="w1b_sb")
+        nc.sync.dma_start(w1b_sb[:], w1b.rearrange("(db p) c -> p db c", p=P))
 
-        dist_sb, cut_sb, table_sb = {}, {}, []
+        dist_sb, cut_sb = {}, {}
         for ch in range(CHUNKS):
             cols = slice(ch * W, (ch + 1) * W)
             for g in range(GROUPS):
@@ -51,15 +51,15 @@ def tile_nodescalarfeatinit_kernel(tc, table, nb, dist, cut, relw, w1b, b1, offs
                 dist_sb[ch, g] = held.tile([P, TG, W], F32, name=f"dist{ch}_{g}")
                 nc.sync.dma_start(dist_sb[ch, g][:], dist_rows[:, blocks, cols])
                 cut_sb[ch, g] = held.tile([P, TG, W], F32, name=f"cut{ch}_{g}")
-                nc.scalar.dma_start(cut_sb[ch, g][:], cut_rows[:, blocks, cols])
-            if ch == 0:
-                for cb, queue in zip(range(CB), (nc.sync, nc.scalar)):
-                    table_sb.append(held.tile([P, S], F32, name=f"table{cb}"))
-                    queue.dma_start(table_sb[cb][:], table[cb * P : (cb + 1) * P, :])
+                nc.sync.dma_start(cut_sb[ch, g][:], cut_rows[:, blocks, cols])
 
+        table_sb = []
+        for cb in range(CB):
+            table_sb.append(held.tile([P, S], F32, name=f"table{cb}"))
+            nc.sync.dma_start(table_sb[cb][:], table[cb * P : (cb + 1) * P, :])
+
+        q_sb = {}
         for ch in range(CHUNKS):
-            cols = slice(ch * W, (ch + 1) * W)
-
             nf_ps = [nf_banks.tile([P, W], F32, name=f"nf_ps{db}") for db in range(CB)]
             for g in range(GROUPS):
                 e = held.tile([P, TG, W], BF16, name=f"e{ch}_{g}")
@@ -90,10 +90,12 @@ def tile_nodescalarfeatinit_kernel(tc, table, nb, dist, cut, relw, w1b, b1, offs
                         start=(db == 0),
                         stop=(db == CB - 1),
                     )
-                q_sb = held.tile([P, W], F32, name=f"q{ch}_{cb}")
-                nc.scalar.activation(q_sb[:], q_ps[:], IDENTITY, bias=b1_sb[:, cb : cb + 1])
+                q_sb[ch, cb] = held.tile([P, W], F32, name=f"q{ch}_{cb}")
+                nc.scalar.activation(q_sb[ch, cb][:], q_ps[:], IDENTITY, bias=b1_sb[:, cb : cb + 1])
 
+        for cb in range(CB):
+            for ch in range(CHUNKS):
                 picked = table_sb[cb][:].indirect(offsets[:, ch * (W // 16) : (ch + 1) * (W // 16)])
                 res = held.tile([P, W], F32, name=f"res{ch}_{cb}")
-                nc.vector.tensor_tensor(res[:], picked, q_sb[:], ADD)
-                nc.sync.dma_start(out[cb * P : (cb + 1) * P, cols], res[:])
+                nc.vector.tensor_tensor(res[:], picked, q_sb[ch, cb][:], ADD)
+                nc.sync.dma_start(out[cb * P : (cb + 1) * P, ch * W : (ch + 1) * W], res[:])

@@ -13,23 +13,20 @@ S = 2048
 N = 1024
 CB = C // P
 TB = N // P
-W = 256
-CHUNKS = N // W
-TG = 4
-GROUPS = TB // TG
+W = 512
+PIECES = N // W
 
 FLOPS = 2 * N * N * C + 2 * C * C * N
 
 
 def tile_nodescalarfeatinit_kernel(tc, table, nb, dist, cut, relw, w1b, b1, offs, out):
     nc = tc.nc
-    dist_rows = dist.rearrange("(tb p) j -> p tb j", p=P)
-    cut_rows = cut.rearrange("(tb p) j -> p tb j", p=P)
+    dist_rows = dist.rearrange("(p r) j -> p r j", r=TB)
+    cut_rows = cut.rearrange("(p r) j -> p r j", r=TB)
 
     with (
         tc.tile_pool(name="held", bufs=1) as held,
-        tc.psum_pool(name="nf_banks", bufs=2) as nf_banks,
-        tc.psum_pool(name="q_banks", bufs=4) as q_banks,
+        tc.psum_pool(name="banks", bufs=1) as banks,
     ):
         offsets = held.tile([P, N // 16], U16, name="offsets")
         nc.sync.dma_start(offsets[:], offs)
@@ -39,63 +36,61 @@ def tile_nodescalarfeatinit_kernel(tc, table, nb, dist, cut, relw, w1b, b1, offs
             nc.sync.dma_start(relw_sb[:], relw.rearrange("(db p) o -> p (db o)", p=P))
             nc.sync.dma_start(b1_sb[:], b1.rearrange("(cb p) o -> p (cb o)", p=P))
         nb_sb = held.tile([P, TB, C], BF16, name="nb_sb")
-        nc.sync.dma_start(nb_sb[:], nb.rearrange("(tb p) d -> p tb d", p=P))
+        nc.sync.dma_start(nb_sb[:], nb.rearrange("(p r) d -> p r d", r=TB))
         w1b_sb = held.tile([P, CB, C], BF16, name="w1b_sb")
         nc.sync.dma_start(w1b_sb[:], w1b.rearrange("(db p) c -> p db c", p=P))
 
-        dist_sb, cut_sb = {}, {}
-        for ch in range(CHUNKS):
-            cols = slice(ch * W, (ch + 1) * W)
-            for g in range(GROUPS):
-                blocks = slice(g * TG, (g + 1) * TG)
-                dist_sb[ch, g] = held.tile([P, TG, W], F32, name=f"dist{ch}_{g}")
-                nc.sync.dma_start(dist_sb[ch, g][:], dist_rows[:, blocks, cols])
-                cut_sb[ch, g] = held.tile([P, TG, W], F32, name=f"cut{ch}_{g}")
-                nc.sync.dma_start(cut_sb[ch, g][:], cut_rows[:, blocks, cols])
+        dist_sb, cut_sb = [], []
+        for r in range(TB):
+            dist_sb.append(held.tile([P, N], F32, name=f"dist{r}"))
+            nc.sync.dma_start(dist_sb[r][:], dist_rows[:, r, :])
+            cut_sb.append(held.tile([P, N], F32, name=f"cut{r}"))
+            nc.sync.dma_start(cut_sb[r][:], cut_rows[:, r, :])
 
         table_sb = []
         for cb in range(CB):
             table_sb.append(held.tile([P, S], F32, name=f"table{cb}"))
             nc.sync.dma_start(table_sb[cb][:], table[cb * P : (cb + 1) * P, :])
 
-        q_sb = {}
-        for ch in range(CHUNKS):
-            nf_ps = [nf_banks.tile([P, W], F32, name=f"nf_ps{db}") for db in range(CB)]
-            for g in range(GROUPS):
-                e = held.tile([P, TG, W], BF16, name=f"e{ch}_{g}")
-                for k in range(TG):
-                    tb = g * TG + k
-                    nc.vector.tensor_tensor(e[:, k, :], dist_sb[ch, g][:, k, :], cut_sb[ch, g][:, k, :], MULT)
-                    for db in range(CB):
-                        nc.tensor.matmul(
-                            nf_ps[db][:],
-                            nb_sb[:, tb, db * P : (db + 1) * P],
-                            e[:, k, :],
-                            start=(tb == 0),
-                            stop=(tb == TB - 1),
-                        )
+        nf_ps = {}
+        for db in range(CB):
+            for h in range(PIECES):
+                nf_ps[db, h] = banks.tile([P, W], F32, name=f"nf_ps{db}_{h}")
+        for r in range(TB):
+            e = held.tile([P, N], BF16, name=f"e{r}")
+            for h in range(PIECES):
+                cols = slice(h * W, (h + 1) * W)
+                nc.vector.tensor_tensor(e[:, cols], dist_sb[r][:, cols], cut_sb[r][:, cols], MULT)
+                for db in range(CB):
+                    nc.tensor.matmul(
+                        nf_ps[db, h][:],
+                        nb_sb[:, r, db * P : (db + 1) * P],
+                        e[:, cols],
+                        start=(r == 0),
+                        stop=(r == TB - 1),
+                    )
 
-            nf_sb = []
-            for db in range(CB):
-                nf_sb.append(held.tile([P, W], BF16, name=f"nf{ch}_{db}"))
-                nc.scalar.activation(nf_sb[db][:], nf_ps[db][:], IDENTITY, scale=relw_sb[:, db : db + 1])
+        nf_sb = {}
+        for h in range(PIECES):
+            nf_sb[0, h] = held.tile([P, W], BF16, name=f"nf0_{h}")
+            nc.scalar.activation(nf_sb[0, h][:], nf_ps[0, h][:], IDENTITY, scale=relw_sb[:, 0:1])
+            nf_sb[1, h] = held.tile([P, W], BF16, name=f"nf1_{h}")
+            nc.vector.tensor_scalar_mul(nf_sb[1, h][:], nf_ps[1, h][:], relw_sb[:, 1:2])
 
-            for cb in range(CB):
-                q_ps = q_banks.tile([P, W], F32, name="q_ps")
+        for cb in range(CB):
+            for h in range(PIECES):
+                q_ps = banks.tile([P, W], F32, name=f"q_ps{cb}_{h}")
                 for db in range(CB):
                     nc.tensor.matmul(
                         q_ps[:],
                         w1b_sb[:, db, cb * P : (cb + 1) * P],
-                        nf_sb[db][:],
+                        nf_sb[db, h][:],
                         start=(db == 0),
                         stop=(db == CB - 1),
                     )
-                q_sb[ch, cb] = held.tile([P, W], F32, name=f"q{ch}_{cb}")
-                nc.scalar.activation(q_sb[ch, cb][:], q_ps[:], IDENTITY, bias=b1_sb[:, cb : cb + 1])
-
-        for cb in range(CB):
-            for ch in range(CHUNKS):
-                picked = table_sb[cb][:].indirect(offsets[:, ch * (W // 16) : (ch + 1) * (W // 16)])
-                res = held.tile([P, W], F32, name=f"res{ch}_{cb}")
-                nc.vector.tensor_tensor(res[:], picked, q_sb[ch, cb][:], ADD)
-                nc.sync.dma_start(out[cb * P : (cb + 1) * P, ch * W : (ch + 1) * W], res[:])
+                q_sb = held.tile([P, W], F32, name=f"q{cb}_{h}")
+                nc.scalar.activation(q_sb[:], q_ps[:], IDENTITY, bias=b1_sb[:, cb : cb + 1])
+                picked = table_sb[cb][:].indirect(offsets[:, h * (W // 16) : (h + 1) * (W // 16)])
+                res = held.tile([P, W], F32, name=f"res{cb}_{h}")
+                nc.vector.tensor_tensor(res[:], picked, q_sb[:], ADD)
+                nc.sync.dma_start(out[cb * P : (cb + 1) * P, h * W : (h + 1) * W], res[:])

@@ -33,19 +33,19 @@ def tile_nodescalarfeatinit_kernel(tc, table, nb, dist, cut, relw, w1b, b1, offs
         relw_sb = held.tile([P, CB], F32, name="relw_sb")
         b1_sb = held.tile([P, CB], F32, name="b1_sb")
         with nc.allow_non_contiguous_dma(reason="one float32 to a partition, 256 in all"):
-            nc.sync.dma_start(relw_sb[:], relw.rearrange("(db p) o -> p (db o)", p=P))
-            nc.sync.dma_start(b1_sb[:], b1.rearrange("(cb p) o -> p (cb o)", p=P))
+            nc.scalar.dma_start(relw_sb[:], relw.rearrange("(db p) o -> p (db o)", p=P))
+            nc.scalar.dma_start(b1_sb[:], b1.rearrange("(cb p) o -> p (cb o)", p=P))
         nb_sb = held.tile([P, TB, C], BF16, name="nb_sb")
         nc.sync.dma_start(nb_sb[:], nb.rearrange("(p r) d -> p r d", r=TB))
         w1b_sb = held.tile([P, CB, C], BF16, name="w1b_sb")
-        nc.sync.dma_start(w1b_sb[:], w1b.rearrange("(db p) c -> p db c", p=P))
+        nc.scalar.dma_start(w1b_sb[:], w1b.rearrange("(db p) c -> p db c", p=P))
 
         dist_sb, cut_sb = [], []
         for r in range(TB):
             dist_sb.append(held.tile([P, N], F32, name=f"dist{r}"))
             nc.sync.dma_start(dist_sb[r][:], dist_rows[:, r, :])
             cut_sb.append(held.tile([P, N], F32, name=f"cut{r}"))
-            nc.sync.dma_start(cut_sb[r][:], cut_rows[:, r, :])
+            nc.scalar.dma_start(cut_sb[r][:], cut_rows[:, r, :])
 
         table_sb = []
         for cb in range(CB):

@@ -13,8 +13,12 @@ S = 2048
 N = 1024
 CB = C // P
 TB = N // P
-W = 512
-PIECES = N // W
+ROWS_OF_LOAD = (2, 2, 2, 1, 1)
+assert sum(ROWS_OF_LOAD) == TB
+BANK = 512
+BANKS = N // BANK
+PIECE = 512
+PIECES = N // PIECE
 
 FLOPS = 2 * N * N * C + 2 * C * C * N
 
@@ -26,71 +30,74 @@ def tile_nodescalarfeatinit_kernel(tc, table, nb, dist, cut, relw, w1b, b1, offs
 
     with (
         tc.tile_pool(name="held", bufs=1) as held,
-        tc.psum_pool(name="banks", bufs=1) as banks,
+        tc.psum_pool(name="nf_banks", bufs=1) as nf_banks,
+        tc.psum_pool(name="q_banks", bufs=4) as q_banks,
     ):
         offsets = held.tile([P, N // 16], U16, name="offsets")
         nc.sync.dma_start(offsets[:], offs)
         relw_sb = held.tile([P, CB], F32, name="relw_sb")
         b1_sb = held.tile([P, CB], F32, name="b1_sb")
         with nc.allow_non_contiguous_dma(reason="one float32 to a partition, 256 in all"):
-            nc.scalar.dma_start(relw_sb[:], relw.rearrange("(db p) o -> p (db o)", p=P))
-            nc.scalar.dma_start(b1_sb[:], b1.rearrange("(cb p) o -> p (cb o)", p=P))
+            nc.sync.dma_start(relw_sb[:], relw.rearrange("(db p) o -> p (db o)", p=P))
+            nc.sync.dma_start(b1_sb[:], b1.rearrange("(cb p) o -> p (cb o)", p=P))
         nb_sb = held.tile([P, TB, C], BF16, name="nb_sb")
         nc.sync.dma_start(nb_sb[:], nb.rearrange("(p r) d -> p r d", r=TB))
         w1b_sb = held.tile([P, CB, C], BF16, name="w1b_sb")
-        nc.scalar.dma_start(w1b_sb[:], w1b.rearrange("(db p) c -> p db c", p=P))
+        nc.sync.dma_start(w1b_sb[:], w1b.rearrange("(db p) c -> p db c", p=P))
 
         dist_sb, cut_sb = [], []
-        for r in range(TB):
-            dist_sb.append(held.tile([P, N], F32, name=f"dist{r}"))
-            nc.sync.dma_start(dist_sb[r][:], dist_rows[:, r, :])
-            cut_sb.append(held.tile([P, N], F32, name=f"cut{r}"))
-            nc.scalar.dma_start(cut_sb[r][:], cut_rows[:, r, :])
+        first_row = 0
+        for g, rows in enumerate(ROWS_OF_LOAD):
+            dist_sb.append(held.tile([P, rows, N], F32, name=f"dist{g}"))
+            nc.sync.dma_start(dist_sb[g][:], dist_rows[:, first_row : first_row + rows, :])
+            cut_sb.append(held.tile([P, rows, N], F32, name=f"cut{g}"))
+            nc.sync.dma_start(cut_sb[g][:], cut_rows[:, first_row : first_row + rows, :])
+            first_row += rows
 
         table_sb = []
         for cb in range(CB):
             table_sb.append(held.tile([P, S], F32, name=f"table{cb}"))
             nc.sync.dma_start(table_sb[cb][:], table[cb * P : (cb + 1) * P, :])
 
-        nf_ps = {}
-        for db in range(CB):
-            for h in range(PIECES):
-                nf_ps[db, h] = banks.tile([P, W], F32, name=f"nf_ps{db}_{h}")
-        for r in range(TB):
-            e = held.tile([P, N], BF16, name=f"e{r}")
-            for h in range(PIECES):
-                cols = slice(h * W, (h + 1) * W)
-                nc.vector.tensor_tensor(e[:, cols], dist_sb[r][:, cols], cut_sb[r][:, cols], MULT)
-                for db in range(CB):
-                    nc.tensor.matmul(
-                        nf_ps[db, h][:],
-                        nb_sb[:, r, db * P : (db + 1) * P],
-                        e[:, cols],
-                        start=(r == 0),
-                        stop=(r == TB - 1),
-                    )
+        nf_ps = [nf_banks.tile([P, N], F32, name=f"nf_ps{db}") for db in range(CB)]
+        r = 0
+        for g, rows in enumerate(ROWS_OF_LOAD):
+            e = held.tile([P, rows, N], BF16, name=f"e{g}")
+            for k in range(rows):
+                for h in range(BANKS):
+                    cols = slice(h * BANK, (h + 1) * BANK)
+                    nc.vector.tensor_tensor(e[:, k, cols], dist_sb[g][:, k, cols], cut_sb[g][:, k, cols], MULT)
+                    for db in range(CB):
+                        nc.tensor.matmul(
+                            nf_ps[db][:, cols],
+                            nb_sb[:, r, db * P : (db + 1) * P],
+                            e[:, k, cols],
+                            start=(r == 0),
+                            stop=(r == TB - 1),
+                        )
+                r += 1
 
-        nf_sb = {}
-        for h in range(PIECES):
-            nf_sb[0, h] = held.tile([P, W], BF16, name=f"nf0_{h}")
-            nc.scalar.activation(nf_sb[0, h][:], nf_ps[0, h][:], IDENTITY, scale=relw_sb[:, 0:1])
-            nf_sb[1, h] = held.tile([P, W], BF16, name=f"nf1_{h}")
-            nc.vector.tensor_scalar_mul(nf_sb[1, h][:], nf_ps[1, h][:], relw_sb[:, 1:2])
+        nf_sb = [held.tile([P, N], BF16, name=f"nf_sb{db}") for db in range(CB)]
+        for i in range(PIECES):
+            cols = slice(i * PIECE, (i + 1) * PIECE)
+            nc.scalar.activation(nf_sb[0][:, cols], nf_ps[0][:, cols], IDENTITY, scale=relw_sb[:, 0:1])
+            nc.vector.tensor_scalar_mul(nf_sb[1][:, cols], nf_ps[1][:, cols], relw_sb[:, 1:2])
 
         for cb in range(CB):
-            for h in range(PIECES):
-                q_ps = banks.tile([P, W], F32, name=f"q_ps{cb}_{h}")
+            for i in range(PIECES):
+                cols = slice(i * PIECE, (i + 1) * PIECE)
+                q_ps = q_banks.tile([P, PIECE], F32, name="q_ps")
                 for db in range(CB):
                     nc.tensor.matmul(
                         q_ps[:],
                         w1b_sb[:, db, cb * P : (cb + 1) * P],
-                        nf_sb[db, h][:],
+                        nf_sb[db][:, cols],
                         start=(db == 0),
                         stop=(db == CB - 1),
                     )
-                q_sb = held.tile([P, W], F32, name=f"q{cb}_{h}")
+                q_sb = held.tile([P, PIECE], F32, name=f"q{cb}_{i}")
                 nc.scalar.activation(q_sb[:], q_ps[:], IDENTITY, bias=b1_sb[:, cb : cb + 1])
-                picked = table_sb[cb][:].indirect(offsets[:, h * (W // 16) : (h + 1) * (W // 16)])
-                res = held.tile([P, W], F32, name=f"res{cb}_{h}")
+                picked = table_sb[cb][:].indirect(offsets[:, i * (PIECE // 16) : (i + 1) * (PIECE // 16)])
+                res = held.tile([P, PIECE], F32, name=f"res{cb}_{i}")
                 nc.vector.tensor_tensor(res[:], picked, q_sb[:], ADD)
-                nc.sync.dma_start(out[cb * P : (cb + 1) * P, h * W : (h + 1) * W], res[:])
+                nc.sync.dma_start(out[cb * P : (cb + 1) * P, cols], res[:])

@@ -13,10 +13,9 @@ S = 2048
 N = 1024
 CB = C // P
 TB = N // P
-ROWS_OF_LOAD = (2, 2, 2, 1, 1)
-assert sum(ROWS_OF_LOAD) == TB
 BANK = 512
 BANKS = N // BANK
+SPANS = [(r, 0, N) for r in range(TB - 1)] + [(TB - 1, h * BANK, (h + 1) * BANK) for h in range(BANKS)]
 PIECE = 512
 PIECES = N // PIECE
 
@@ -46,42 +45,40 @@ def tile_nodescalarfeatinit_kernel(tc, table, nb, dist, cut, relw, w1b, b1, offs
         nc.sync.dma_start(w1b_sb[:], w1b.rearrange("(db p) c -> p db c", p=P))
 
         dist_sb, cut_sb = [], []
-        first_row = 0
-        for g, rows in enumerate(ROWS_OF_LOAD):
-            dist_sb.append(held.tile([P, rows, N], F32, name=f"dist{g}"))
-            nc.sync.dma_start(dist_sb[g][:], dist_rows[:, first_row : first_row + rows, :])
-            cut_sb.append(held.tile([P, rows, N], F32, name=f"cut{g}"))
-            nc.sync.dma_start(cut_sb[g][:], cut_rows[:, first_row : first_row + rows, :])
-            first_row += rows
+        for r, lo, hi in SPANS:
+            dist_sb.append(held.tile([P, hi - lo], F32, name=f"dist{r}_{lo}"))
+            nc.sync.dma_start(dist_sb[-1][:], dist_rows[:, r, lo:hi])
+            cut_sb.append(held.tile([P, hi - lo], F32, name=f"cut{r}_{lo}"))
+            nc.sync.dma_start(cut_sb[-1][:], cut_rows[:, r, lo:hi])
 
         table_sb = []
         for cb in range(CB):
             table_sb.append(held.tile([P, S], F32, name=f"table{cb}"))
             nc.sync.dma_start(table_sb[cb][:], table[cb * P : (cb + 1) * P, :])
 
-        nf_ps = [nf_banks.tile([P, N], F32, name=f"nf_ps{db}") for db in range(CB)]
-        r = 0
-        for g, rows in enumerate(ROWS_OF_LOAD):
-            e = held.tile([P, rows, N], BF16, name=f"e{g}")
-            for k in range(rows):
-                for h in range(BANKS):
-                    cols = slice(h * BANK, (h + 1) * BANK)
-                    nc.vector.tensor_tensor(e[:, k, cols], dist_sb[g][:, k, cols], cut_sb[g][:, k, cols], MULT)
-                    for db in range(CB):
-                        nc.tensor.matmul(
-                            nf_ps[db][:, cols],
-                            nb_sb[:, r, db * P : (db + 1) * P],
-                            e[:, k, cols],
-                            start=(r == 0),
-                            stop=(r == TB - 1),
-                        )
-                r += 1
+        nf_ps = {}
+        for db in range(CB):
+            for first in range(0, N, BANK):
+                nf_ps[db, first] = nf_banks.tile([P, BANK], F32, name=f"nf_ps{db}_{first}")
+        for (r, lo, hi), dist_span, cut_span in zip(SPANS, dist_sb, cut_sb):
+            e = held.tile([P, hi - lo], BF16, name=f"e{r}_{lo}")
+            for first in range(lo, hi, BANK):
+                here = slice(first - lo, first - lo + BANK)
+                nc.vector.tensor_tensor(e[:, here], dist_span[:, here], cut_span[:, here], MULT)
+                for db in range(CB):
+                    nc.tensor.matmul(
+                        nf_ps[db, first][:],
+                        nb_sb[:, r, db * P : (db + 1) * P],
+                        e[:, here],
+                        start=(r == 0),
+                        stop=(r == TB - 1),
+                    )
 
         nf_sb = [held.tile([P, N], BF16, name=f"nf_sb{db}") for db in range(CB)]
-        for i in range(PIECES):
-            cols = slice(i * PIECE, (i + 1) * PIECE)
-            nc.scalar.activation(nf_sb[0][:, cols], nf_ps[0][:, cols], IDENTITY, scale=relw_sb[:, 0:1])
-            nc.vector.tensor_scalar_mul(nf_sb[1][:, cols], nf_ps[1][:, cols], relw_sb[:, 1:2])
+        for first in range(0, N, BANK):
+            cols = slice(first, first + BANK)
+            nc.scalar.activation(nf_sb[0][:, cols], nf_ps[0, first][:], IDENTITY, scale=relw_sb[:, 0:1])
+            nc.vector.tensor_scalar_mul(nf_sb[1][:, cols], nf_ps[1, first][:], relw_sb[:, 1:2])
 
         for cb in range(CB):
             for i in range(PIECES):

@@ -15,7 +15,11 @@ CB = C // P
 TB = N // P
 BANK = 512
 BANKS = N // BANK
-SPANS = [(r, 0, N) for r in range(TB - 1)] + [(TB - 1, h * BANK, (h + 1) * BANK) for h in range(BANKS)]
+SPANS = (
+    [(r, 2, 0, N) for r in range(0, TB - 2, 2)]
+    + [(TB - 2, 1, 0, N)]
+    + [(TB - 1, 1, lo, lo + BANK) for lo in range(0, N, BANK)]
+)
 PIECE = 512
 PIECES = N // PIECE
 
@@ -45,11 +49,11 @@ def tile_nodescalarfeatinit_kernel(tc, table, nb, dist, cut, relw, w1b, b1, offs
         nc.sync.dma_start(w1b_sb[:], w1b.rearrange("(db p) c -> p db c", p=P))
 
         dist_sb, cut_sb = [], []
-        for r, lo, hi in SPANS:
-            dist_sb.append(held.tile([P, hi - lo], F32, name=f"dist{r}_{lo}"))
-            nc.sync.dma_start(dist_sb[-1][:], dist_rows[:, r, lo:hi])
-            cut_sb.append(held.tile([P, hi - lo], F32, name=f"cut{r}_{lo}"))
-            nc.sync.dma_start(cut_sb[-1][:], cut_rows[:, r, lo:hi])
+        for r0, rows, lo, hi in SPANS:
+            dist_sb.append(held.tile([P, rows, hi - lo], F32, name=f"dist{r0}_{lo}"))
+            nc.sync.dma_start(dist_sb[-1][:], dist_rows[:, r0 : r0 + rows, lo:hi])
+            cut_sb.append(held.tile([P, rows, hi - lo], F32, name=f"cut{r0}_{lo}"))
+            nc.sync.dma_start(cut_sb[-1][:], cut_rows[:, r0 : r0 + rows, lo:hi])
 
         table_sb = []
         for cb in range(CB):
@@ -60,19 +64,20 @@ def tile_nodescalarfeatinit_kernel(tc, table, nb, dist, cut, relw, w1b, b1, offs
         for db in range(CB):
             for first in range(0, N, BANK):
                 nf_ps[db, first] = nf_banks.tile([P, BANK], F32, name=f"nf_ps{db}_{first}")
-        for (r, lo, hi), dist_span, cut_span in zip(SPANS, dist_sb, cut_sb):
-            e = held.tile([P, hi - lo], BF16, name=f"e{r}_{lo}")
-            for first in range(lo, hi, BANK):
-                here = slice(first - lo, first - lo + BANK)
-                nc.vector.tensor_tensor(e[:, here], dist_span[:, here], cut_span[:, here], MULT)
-                for db in range(CB):
-                    nc.tensor.matmul(
-                        nf_ps[db, first][:],
-                        nb_sb[:, r, db * P : (db + 1) * P],
-                        e[:, here],
-                        start=(r == 0),
-                        stop=(r == TB - 1),
-                    )
+        for (r0, rows, lo, hi), dist_span, cut_span in zip(SPANS, dist_sb, cut_sb):
+            e = held.tile([P, rows, hi - lo], BF16, name=f"e{r0}_{lo}")
+            for k in range(rows):
+                for first in range(lo, hi, BANK):
+                    here = slice(first - lo, first - lo + BANK)
+                    nc.vector.tensor_tensor(e[:, k, here], dist_span[:, k, here], cut_span[:, k, here], MULT)
+                    for db in range(CB):
+                        nc.tensor.matmul(
+                            nf_ps[db, first][:],
+                            nb_sb[:, r0 + k, db * P : (db + 1) * P],
+                            e[:, k, here],
+                            start=(r0 + k == 0),
+                            stop=(r0 + k == TB - 1),
+                        )
 
         nf_sb = [held.tile([P, N], BF16, name=f"nf_sb{db}") for db in range(CB)]
         for first in range(0, N, BANK):

@@ -20,7 +20,7 @@ SPANS = (
     + [(TB - 2, 1, 0, N)]
     + [(TB - 1, 1, lo, lo + BANK) for lo in range(0, N, BANK)]
 )
-PIECE = 512
+PIECE = 256
 PIECES = N // PIECE
 
 FLOPS = 2 * N * N * C + 2 * C * C * N
@@ -80,10 +80,12 @@ def tile_nodescalarfeatinit_kernel(tc, table, nb, dist, cut, relw, w1b, b1, offs
                         )
 
         nf_sb = [held.tile([P, N], BF16, name=f"nf_sb{db}") for db in range(CB)]
-        for first in range(0, N, BANK):
-            cols = slice(first, first + BANK)
-            nc.scalar.activation(nf_sb[0][:, cols], nf_ps[0, first][:], IDENTITY, scale=relw_sb[:, 0:1])
-            nc.vector.tensor_scalar_mul(nf_sb[1][:, cols], nf_ps[1, first][:], relw_sb[:, 1:2])
+        for i in range(PIECES):
+            cols = slice(i * PIECE, (i + 1) * PIECE)
+            first = i * PIECE // BANK * BANK
+            in_bank = slice(i * PIECE - first, (i + 1) * PIECE - first)
+            nc.scalar.activation(nf_sb[0][:, cols], nf_ps[0, first][:, in_bank], IDENTITY, scale=relw_sb[:, 0:1])
+            nc.vector.tensor_scalar_mul(nf_sb[1][:, cols], nf_ps[1, first][:, in_bank], relw_sb[:, 1:2])
 
         for cb in range(CB):
             for i in range(PIECES):

@@ -30,6 +30,8 @@ def tile_nodescalarfeatinit_kernel(tc, table, nb, dist, cut, relw, w1b, b1, offs
     nc = tc.nc
     dist_rows = dist.rearrange("(p r) j -> p r j", r=TB)
     cut_rows = cut.rearrange("(p r) j -> p r j", r=TB)
+    table_blocks = table.rearrange("(p cb) s -> p cb s", cb=CB)
+    out_blocks = out.rearrange("(p cb) j -> p cb j", cb=CB)
 
     with (
         tc.tile_pool(name="held", bufs=1) as held,
@@ -40,13 +42,13 @@ def tile_nodescalarfeatinit_kernel(tc, table, nb, dist, cut, relw, w1b, b1, offs
         nc.sync.dma_start(offsets[:], offs)
         relw_sb = held.tile([P, CB], F32, name="relw_sb")
         b1_sb = held.tile([P, CB], F32, name="b1_sb")
-        with nc.allow_non_contiguous_dma(reason="one float32 to a partition, 256 in all"):
-            nc.sync.dma_start(relw_sb[:], relw.rearrange("(db p) o -> p (db o)", p=P))
-            nc.sync.dma_start(b1_sb[:], b1.rearrange("(cb p) o -> p (cb o)", p=P))
-        nb_sb = held.tile([P, TB, C], BF16, name="nb_sb")
-        nc.sync.dma_start(nb_sb[:], nb.rearrange("(p r) d -> p r d", r=TB))
-        w1b_sb = held.tile([P, CB, C], BF16, name="w1b_sb")
-        nc.sync.dma_start(w1b_sb[:], w1b.rearrange("(db p) c -> p db c", p=P))
+        with nc.allow_non_contiguous_dma(reason="two float32 to a partition, 256 in all"):
+            nc.sync.dma_start(relw_sb[:], relw.rearrange("(p db) o -> p (db o)", p=P))
+            nc.sync.dma_start(b1_sb[:], b1.rearrange("(p cb) o -> p (cb o)", p=P))
+        nb_sb = held.tile([P, TB, P, CB], BF16, name="nb_sb")
+        nc.sync.dma_start(nb_sb[:], nb.rearrange("(p r) (m db) -> p r m db", r=TB, db=CB))
+        w1b_sb = held.tile([P, CB, P, CB], BF16, name="w1b_sb")
+        nc.sync.dma_start(w1b_sb[:], w1b.rearrange("(p db) (m cb) -> p db m cb", db=CB, cb=CB))
 
         dist_sb, cut_sb = [], []
         for r0, rows, lo, hi in SPANS:
@@ -58,7 +60,7 @@ def tile_nodescalarfeatinit_kernel(tc, table, nb, dist, cut, relw, w1b, b1, offs
         table_sb = []
         for cb in range(CB):
             table_sb.append(held.tile([P, S], F32, name=f"table{cb}"))
-            nc.sync.dma_start(table_sb[cb][:], table[cb * P : (cb + 1) * P, :])
+            nc.sync.dma_start(table_sb[cb][:], table_blocks[:, cb, :])
 
         nf_ps = {}
         for db in range(CB):
@@ -73,7 +75,7 @@ def tile_nodescalarfeatinit_kernel(tc, table, nb, dist, cut, relw, w1b, b1, offs
                     for db in range(CB):
                         nc.tensor.matmul(
                             nf_ps[db, first][:],
-                            nb_sb[:, r0 + k, db * P : (db + 1) * P],
+                            nb_sb[:, r0 + k, :, db],
                             e[:, k, here],
                             start=(r0 + k == 0),
                             stop=(r0 + k == TB - 1),
@@ -94,7 +96,7 @@ def tile_nodescalarfeatinit_kernel(tc, table, nb, dist, cut, relw, w1b, b1, offs
                 for db in range(CB):
                     nc.tensor.matmul(
                         q_ps[:],
-                        w1b_sb[:, db, cb * P : (cb + 1) * P],
+                        w1b_sb[:, db, :, cb],
                         nf_sb[db][:, cols],
                         start=(db == 0),
                         stop=(db == CB - 1),
@@ -104,4 +106,4 @@ def tile_nodescalarfeatinit_kernel(tc, table, nb, dist, cut, relw, w1b, b1, offs
                 picked = table_sb[cb][:].indirect(offsets[:, i * (PIECE // 16) : (i + 1) * (PIECE // 16)])
                 res = held.tile([P, PIECE], F32, name=f"res{cb}_{i}")
                 nc.vector.tensor_tensor(res[:], picked, q_sb[:], ADD)
-                nc.sync.dma_start(out[cb * P : (cb + 1) * P, cols], res[:])
+                nc.sync.dma_start(out_blocks[:, cb, cols], res[:])

@@ -38,17 +38,11 @@ def tile_nodescalarfeatinit_kernel(tc, table, nb, dist, cut, relw, w1b, b1, offs
         tc.psum_pool(name="nf_banks", bufs=1) as nf_banks,
         tc.psum_pool(name="q_banks", bufs=4) as q_banks,
     ):
-        offsets = held.tile([P, N // 16], U16, name="offsets")
-        nc.sync.dma_start(offsets[:], offs)
         relw_sb = held.tile([P, CB], F32, name="relw_sb")
-        b1_sb = held.tile([P, CB], F32, name="b1_sb")
         with nc.allow_non_contiguous_dma(reason="two float32 to a partition, 256 in all"):
             nc.sync.dma_start(relw_sb[:], relw.rearrange("(p db) o -> p (db o)", p=P))
-            nc.sync.dma_start(b1_sb[:], b1.rearrange("(p cb) o -> p (cb o)", p=P))
         nb_sb = held.tile([P, TB, P, CB], BF16, name="nb_sb")
         nc.sync.dma_start(nb_sb[:], nb.rearrange("(p r) (m db) -> p r m db", r=TB, db=CB))
-        w1b_sb = held.tile([P, CB, P, CB], BF16, name="w1b_sb")
-        nc.sync.dma_start(w1b_sb[:], w1b.rearrange("(p db) (m cb) -> p db m cb", db=CB, cb=CB))
 
         dist_sb, cut_sb = [], []
         for r0, rows, lo, hi in SPANS:
@@ -56,6 +50,14 @@ def tile_nodescalarfeatinit_kernel(tc, table, nb, dist, cut, relw, w1b, b1, offs
             nc.sync.dma_start(dist_sb[-1][:], dist_rows[:, r0 : r0 + rows, lo:hi])
             cut_sb.append(held.tile([P, rows, hi - lo], F32, name=f"cut{r0}_{lo}"))
             nc.sync.dma_start(cut_sb[-1][:], cut_rows[:, r0 : r0 + rows, lo:hi])
+
+        w1b_sb = held.tile([P, CB, P, CB], BF16, name="w1b_sb")
+        nc.sync.dma_start(w1b_sb[:], w1b.rearrange("(p db) (m cb) -> p db m cb", db=CB, cb=CB))
+        b1_sb = held.tile([P, CB], F32, name="b1_sb")
+        with nc.allow_non_contiguous_dma(reason="two float32 to a partition, 256 in all"):
+            nc.sync.dma_start(b1_sb[:], b1.rearrange("(p cb) o -> p (cb o)", p=P))
+        offsets = held.tile([P, N // 16], U16, name="offsets")
+        nc.sync.dma_start(offsets[:], offs)
 
         table_sb = []
         for cb in range(CB):

@@ -70,17 +70,19 @@ def tile_nodescalarfeatinit_kernel(tc, table, nb, dist, cut, relw, w1b, b1, offs
                 nf_ps[db, first] = nf_banks.tile([P, BANK], F32, name=f"nf_ps{db}_{first}")
         for (r0, rows, lo, hi), dist_span, cut_span in zip(SPANS, dist_sb, cut_sb):
             e = held.tile([P, rows, hi - lo], BF16, name=f"e{r0}_{lo}")
+            step = PIECE if r0 == TB - 1 else BANK
             for k in range(rows):
-                for first in range(lo, hi, BANK):
-                    here = slice(first - lo, first - lo + BANK)
+                for at in range(lo, hi, step):
+                    first = at // BANK * BANK
+                    here = slice(at - lo, at - lo + step)
                     nc.vector.tensor_tensor(e[:, k, here], dist_span[:, k, here], cut_span[:, k, here], MULT)
                     for db in range(CB):
                         nc.tensor.matmul(
-                            nf_ps[db, first][:],
+                            nf_ps[db, first][:, at - first : at - first + step],
                             nb_sb[:, r0 + k, :, db],
                             e[:, k, here],
                             start=(r0 + k == 0),
-                            stop=(r0 + k == TB - 1),
+                            stop=(r0 + k == TB - 1 and at + step == first + BANK),
                         )
 
         nf_sb = [held.tile([P, N], BF16, name=f"nf_sb{db}") for db in range(CB)]

@@ -38,9 +38,6 @@ def tile_nodescalarfeatinit_kernel(tc, table, nb, dist, cut, relw, w1b, b1, offs
         tc.psum_pool(name="nf_banks", bufs=1) as nf_banks,
         tc.psum_pool(name="q_banks", bufs=4) as q_banks,
     ):
-        relw_sb = held.tile([P, CB], F32, name="relw_sb")
-        with nc.allow_non_contiguous_dma(reason="two float32 to a partition, 256 in all"):
-            nc.sync.dma_start(relw_sb[:], relw.rearrange("(p db) o -> p (db o)", p=P))
         nb_sb = held.tile([P, TB, P, CB], BF16, name="nb_sb")
         nc.sync.dma_start(nb_sb[:], nb.rearrange("(p r) (m db) -> p r m db", r=TB, db=CB))
 
@@ -50,12 +47,14 @@ def tile_nodescalarfeatinit_kernel(tc, table, nb, dist, cut, relw, w1b, b1, offs
             nc.sync.dma_start(dist_sb[-1][:], dist_rows[:, r0 : r0 + rows, lo:hi])
             cut_sb.append(held.tile([P, rows, hi - lo], F32, name=f"cut{r0}_{lo}"))
             nc.sync.dma_start(cut_sb[-1][:], cut_rows[:, r0 : r0 + rows, lo:hi])
+            if r0 == 0:
+                relw_row = held.tile([1, P, CB], F32, name="relw_row")
+                nc.sync.dma_start(relw_row[:], relw.rearrange("(p db) o -> o p db", db=CB))
+                b1_row = held.tile([1, P, CB], F32, name="b1_row")
+                nc.sync.dma_start(b1_row[:], b1.rearrange("(p cb) o -> o p cb", cb=CB))
 
         w1b_sb = held.tile([P, CB, P, CB], BF16, name="w1b_sb")
         nc.sync.dma_start(w1b_sb[:], w1b.rearrange("(p db) (m cb) -> p db m cb", db=CB, cb=CB))
-        b1_sb = held.tile([P, CB], F32, name="b1_sb")
-        with nc.allow_non_contiguous_dma(reason="two float32 to a partition, 256 in all"):
-            nc.sync.dma_start(b1_sb[:], b1.rearrange("(p cb) o -> p (cb o)", p=P))
         offsets = held.tile([P, N // 16], U16, name="offsets")
         nc.sync.dma_start(offsets[:], offs)
 
@@ -84,6 +83,17 @@ def tile_nodescalarfeatinit_kernel(tc, table, nb, dist, cut, relw, w1b, b1, offs
                             start=(r0 + k == 0),
                             stop=(r0 + k == TB - 1 and at + step == first + BANK),
                         )
+            if r0 == 0:
+                one = held.tile([1, 1], F32, name="one")
+                nc.vector.memset(one[:], 1.0)
+                columns_ps = q_banks.tile([P, PIECE], F32, name="q_ps")
+                for b in range(CB):
+                    nc.tensor.matmul(columns_ps[:, b : b + 1], relw_row[:, :, b], one[:], start=True, stop=True)
+                    nc.tensor.matmul(columns_ps[:, CB + b : CB + b + 1], b1_row[:, :, b], one[:], start=True, stop=True)
+                relw_sb = held.tile([P, CB], F32, name="relw_sb")
+                nc.vector.tensor_copy(relw_sb[:], columns_ps[:, 0:CB])
+                b1_sb = held.tile([P, CB], F32, name="b1_sb")
+                nc.vector.tensor_copy(b1_sb[:], columns_ps[:, CB : 2 * CB])
 
         nf_sb = [held.tile([P, N], BF16, name=f"nf_sb{db}") for db in range(CB)]
         for i in range(PIECES):

@@ -8,6 +8,7 @@ ADD = mybir.AluOpType.add
 IDENTITY = mybir.ActivationFunctionType.Identity
 
 P = 128
+LINE = 256
 C = 256
 S = 2048
 N = 1024
@@ -38,14 +39,14 @@ def tile_nodescalarfeatinit_kernel(tc, table, nb, dist, cut, relw, w1b, b1, offs
         tc.psum_pool(name="nf_banks", bufs=1) as nf_banks,
         tc.psum_pool(name="q_banks", bufs=4) as q_banks,
     ):
-        nb_sb = held.tile([P, TB, P, CB], BF16, name="nb_sb")
+        nb_sb = held.tile([P, TB, P, CB], BF16, name="nb_sb", align_bytes=LINE)
         nc.sync.dma_start(nb_sb[:], nb.rearrange("(p r) (m db) -> p r m db", r=TB, db=CB))
 
         dist_sb, cut_sb = [], []
         for r0, rows, lo, hi in SPANS:
-            dist_sb.append(held.tile([P, rows, hi - lo], F32, name=f"dist{r0}_{lo}"))
+            dist_sb.append(held.tile([P, rows, hi - lo], F32, name=f"dist{r0}_{lo}", align_bytes=LINE))
             nc.sync.dma_start(dist_sb[-1][:], dist_rows[:, r0 : r0 + rows, lo:hi])
-            cut_sb.append(held.tile([P, rows, hi - lo], F32, name=f"cut{r0}_{lo}"))
+            cut_sb.append(held.tile([P, rows, hi - lo], F32, name=f"cut{r0}_{lo}", align_bytes=LINE))
             nc.sync.dma_start(cut_sb[-1][:], cut_rows[:, r0 : r0 + rows, lo:hi])
             if r0 == 0:
                 relw_row = held.tile([1, P, CB], F32, name="relw_row")
@@ -53,14 +54,14 @@ def tile_nodescalarfeatinit_kernel(tc, table, nb, dist, cut, relw, w1b, b1, offs
                 b1_row = held.tile([1, P, CB], F32, name="b1_row")
                 nc.sync.dma_start(b1_row[:], b1.rearrange("(p cb) o -> o p cb", cb=CB))
 
-        w1b_sb = held.tile([P, CB, P, CB], BF16, name="w1b_sb")
+        w1b_sb = held.tile([P, CB, P, CB], BF16, name="w1b_sb", align_bytes=LINE)
         nc.sync.dma_start(w1b_sb[:], w1b.rearrange("(p db) (m cb) -> p db m cb", db=CB, cb=CB))
-        offsets = held.tile([P, N // 16], U16, name="offsets")
+        offsets = held.tile([P, N // 16], U16, name="offsets", align_bytes=LINE)
         nc.sync.dma_start(offsets[:], offs)
 
         table_sb = []
         for cb in range(CB):
-            table_sb.append(held.tile([P, S], F32, name=f"table{cb}"))
+            table_sb.append(held.tile([P, S], F32, name=f"table{cb}", align_bytes=LINE))
             nc.sync.dma_start(table_sb[cb][:], table_blocks[:, cb, :])
 
         nf_ps = {}
@@ -118,6 +119,6 @@ def tile_nodescalarfeatinit_kernel(tc, table, nb, dist, cut, relw, w1b, b1, offs
                 q_sb = held.tile([P, PIECE], F32, name=f"q{cb}_{i}")
                 nc.scalar.activation(q_sb[:], q_ps[:], IDENTITY, bias=b1_sb[:, cb : cb + 1])
                 picked = table_sb[cb][:].indirect(offsets[:, i * (PIECE // 16) : (i + 1) * (PIECE // 16)])
-                res = held.tile([P, PIECE], F32, name=f"res{cb}_{i}")
+                res = held.tile([P, PIECE], F32, name=f"res{cb}_{i}", align_bytes=LINE)
                 nc.vector.tensor_tensor(res[:], picked, q_sb[:], ADD)
                 nc.sync.dma_start(out_blocks[:, cb, cols], res[:])

@@ -29,8 +29,9 @@ FLOPS = 2 * N * N * C + 2 * C * C * N
 
 def tile_nodescalarfeatinit_kernel(tc, table, nb, dist, cut, relw, w1b, b1, offs, out):
     nc = tc.nc
-    dist_rows = dist.rearrange("(p r) j -> p r j", r=TB)
-    cut_rows = cut.rearrange("(p r) j -> p r j", r=TB)
+    def span_rows(array, r0, rows):
+        return array[r0 * P : (r0 + rows) * P, :].rearrange("(p k) j -> p k j", k=rows)
+
     table_blocks = table.rearrange("(p cb) s -> p cb s", cb=CB)
     out_blocks = out.rearrange("(p cb) j -> p cb j", cb=CB)
 
@@ -40,14 +41,22 @@ def tile_nodescalarfeatinit_kernel(tc, table, nb, dist, cut, relw, w1b, b1, offs
         tc.psum_pool(name="q_banks", bufs=4) as q_banks,
     ):
         nb_sb = held.tile([P, TB, P, CB], BF16, name="nb_sb", align_bytes=LINE)
-        nc.sync.dma_start(nb_sb[:], nb.rearrange("(p r) (m db) -> p r m db", r=TB, db=CB))
+        paired = TB - 2
+        nc.sync.dma_start(
+            nb_sb[:, :paired, :, :].rearrange("p (s k) m db -> p s (k m db)", k=2),
+            nb[: paired * P, :].rearrange("(s p k) d -> p s (k d)", p=P, k=2),
+        )
+        nc.sync.dma_start(
+            nb_sb[:, paired:, :, :].rearrange("p s m db -> p s (m db)"),
+            nb[paired * P :, :].rearrange("(s p) d -> p s d", p=P),
+        )
 
         dist_sb, cut_sb = [], []
         for r0, rows, lo, hi in SPANS:
             dist_sb.append(held.tile([P, rows, hi - lo], F32, name=f"dist{r0}_{lo}", align_bytes=LINE))
-            nc.sync.dma_start(dist_sb[-1][:], dist_rows[:, r0 : r0 + rows, lo:hi])
+            nc.sync.dma_start(dist_sb[-1][:], span_rows(dist, r0, rows)[:, :, lo:hi])
             cut_sb.append(held.tile([P, rows, hi - lo], F32, name=f"cut{r0}_{lo}", align_bytes=LINE))
-            nc.sync.dma_start(cut_sb[-1][:], cut_rows[:, r0 : r0 + rows, lo:hi])
+            nc.sync.dma_start(cut_sb[-1][:], span_rows(cut, r0, rows)[:, :, lo:hi])
             if r0 == 0:
                 relw_row = held.tile([1, P, CB], F32, name="relw_row")
                 nc.sync.dma_start(relw_row[:], relw.rearrange("(p db) o -> o p db", db=CB))

import concourse.mybir as mybir

F32 = mybir.dt.float32
BF16 = mybir.dt.bfloat16
U16 = mybir.dt.uint16
MULT = mybir.AluOpType.mult
ADD = mybir.AluOpType.add
IDENTITY = mybir.ActivationFunctionType.Identity

P = 128
LINE = 256
C = 256
S = 2048
N = 1024
CB = C // P
TB = N // P
BANK = 512
BANKS = N // BANK
SPANS = (
    [(r, 2, 0, N) for r in range(0, TB - 2, 2)]
    + [(TB - 2, 1, 0, N)]
    + [(TB - 1, 1, lo, lo + BANK) for lo in range(0, N, BANK)]
)
PIECE = 256
PIECES = N // PIECE

FLOPS = 2 * N * N * C + 2 * C * C * N


def tile_nodescalarfeatinit_kernel(tc, table, nb, dist, cut, relw, w1b, b1, offs, out):
    nc = tc.nc
    def span_rows(array, r0, rows):
        return array[r0 * P : (r0 + rows) * P, :].rearrange("(p k) j -> p k j", k=rows)

    table_blocks = table.rearrange("(p cb) s -> p cb s", cb=CB)
    out_blocks = out.rearrange("(p cb) j -> p cb j", cb=CB)

    with (
        tc.tile_pool(name="held", bufs=1) as held,
        tc.psum_pool(name="nf_banks", bufs=1) as nf_banks,
        tc.psum_pool(name="q_banks", bufs=4) as q_banks,
    ):
        nb_sb = held.tile([P, TB, P, CB], BF16, name="nb_sb", align_bytes=LINE)
        paired = TB - 2
        nc.sync.dma_start(
            nb_sb[:, :paired, :, :].rearrange("p (s k) m db -> p s (k m db)", k=2),
            nb[: paired * P, :].rearrange("(s p k) d -> p s (k d)", p=P, k=2),
        )
        nc.sync.dma_start(
            nb_sb[:, paired:, :, :].rearrange("p s m db -> p s (m db)"),
            nb[paired * P :, :].rearrange("(s p) d -> p s d", p=P),
        )

        dist_sb, cut_sb = [], []
        for r0, rows, lo, hi in SPANS:
            dist_sb.append(held.tile([P, rows, hi - lo], F32, name=f"dist{r0}_{lo}", align_bytes=LINE))
            nc.sync.dma_start(dist_sb[-1][:], span_rows(dist, r0, rows)[:, :, lo:hi])
            cut_sb.append(held.tile([P, rows, hi - lo], F32, name=f"cut{r0}_{lo}", align_bytes=LINE))
            nc.sync.dma_start(cut_sb[-1][:], span_rows(cut, r0, rows)[:, :, lo:hi])
            if r0 == 0:
                relw_row = held.tile([1, P, CB], F32, name="relw_row")
                nc.sync.dma_start(relw_row[:], relw.rearrange("(p db) o -> o p db", db=CB))
                b1_row = held.tile([1, P, CB], F32, name="b1_row")
                nc.sync.dma_start(b1_row[:], b1.rearrange("(p cb) o -> o p cb", cb=CB))

        w1b_sb = held.tile([P, CB, P, CB], BF16, name="w1b_sb", align_bytes=LINE)
        nc.sync.dma_start(w1b_sb[:], w1b.rearrange("(p db) (m cb) -> p db m cb", db=CB, cb=CB))
        offsets = held.tile([P, N // 16], U16, name="offsets", align_bytes=LINE)
        nc.sync.dma_start(offsets[:], offs)

        table_sb = []
        for cb in range(CB):
            table_sb.append(held.tile([P, S], F32, name=f"table{cb}", align_bytes=LINE))
            nc.sync.dma_start(table_sb[cb][:], table_blocks[:, cb, :])

        nf_ps = {}
        for db in range(CB):
            for first in range(0, N, BANK):
                nf_ps[db, first] = nf_banks.tile([P, BANK], F32, name=f"nf_ps{db}_{first}")
        for (r0, rows, lo, hi), dist_span, cut_span in zip(SPANS, dist_sb, cut_sb):
            e = held.tile([P, rows, hi - lo], BF16, name=f"e{r0}_{lo}")
            step = PIECE if r0 == TB - 1 else BANK
            for k in range(rows):
                for at in range(lo, hi, step):
                    first = at // BANK * BANK
                    here = slice(at - lo, at - lo + step)
                    nc.vector.tensor_tensor(e[:, k, here], dist_span[:, k, here], cut_span[:, k, here], MULT)
                    for db in range(CB):
                        nc.tensor.matmul(
                            nf_ps[db, first][:, at - first : at - first + step],
                            nb_sb[:, r0 + k, :, db],
                            e[:, k, here],
                            start=(r0 + k == 0),
                            stop=(r0 + k == TB - 1 and at + step == first + BANK),
                        )
            if r0 == 0:
                one = held.tile([1, 1], F32, name="one")
                nc.vector.memset(one[:], 1.0)
                columns_ps = q_banks.tile([P, PIECE], F32, name="q_ps")
                for b in range(CB):
                    nc.tensor.matmul(columns_ps[:, b : b + 1], relw_row[:, :, b], one[:], start=True, stop=True)
                    nc.tensor.matmul(columns_ps[:, CB + b : CB + b + 1], b1_row[:, :, b], one[:], start=True, stop=True)
                relw_sb = held.tile([P, CB], F32, name="relw_sb")
                nc.vector.tensor_copy(relw_sb[:], columns_ps[:, 0:CB])
                b1_sb = held.tile([P, CB], F32, name="b1_sb")
                nc.vector.tensor_copy(b1_sb[:], columns_ps[:, CB : 2 * CB])

        nf_sb = [held.tile([P, N], BF16, name=f"nf_sb{db}") for db in range(CB)]
        for i in range(PIECES):
            cols = slice(i * PIECE, (i + 1) * PIECE)
            first = i * PIECE // BANK * BANK
            in_bank = slice(i * PIECE - first, (i + 1) * PIECE - first)
            nc.scalar.activation(nf_sb[0][:, cols], nf_ps[0, first][:, in_bank], IDENTITY, scale=relw_sb[:, 0:1])
            nc.vector.tensor_scalar_mul(nf_sb[1][:, cols], nf_ps[1, first][:, in_bank], relw_sb[:, 1:2])

        for cb in range(CB):
            for i in range(PIECES):
                cols = slice(i * PIECE, (i + 1) * PIECE)
                q_ps = q_banks.tile([P, PIECE], F32, name="q_ps")
                for db in range(CB):
                    nc.tensor.matmul(
                        q_ps[:],
                        w1b_sb[:, db, :, cb],
                        nf_sb[db][:, cols],
                        start=(db == 0),
                        stop=(db == CB - 1),
                    )
                q_sb = held.tile([P, PIECE], F32, name=f"q{cb}_{i}")
                nc.scalar.activation(q_sb[:], q_ps[:], IDENTITY, bias=b1_sb[:, cb : cb + 1])
                picked = table_sb[cb][:].indirect(offsets[:, i * (PIECE // 16) : (i + 1) * (PIECE // 16)])
                res = held.tile([P, PIECE], F32, name=f"res{cb}_{i}", align_bytes=LINE)
                nc.vector.tensor_tensor(res[:], picked, q_sb[:], ADD)
                nc.sync.dma_start(out_blocks[:, cb, cols], res[:])
